import numpy as np
import ml_dtypes


def mxq(x, axis, fmt="e4m3"):
    dtype, down = {"e4m3": (ml_dtypes.float8_e4m3fn, 7), "e5m2": (ml_dtypes.float8_e5m2, 14)}[fmt]
    v = np.moveaxis(np.asarray(x, np.float32).astype(ml_dtypes.bfloat16).astype(np.float64), axis, -1)
    blocks = v.reshape(v.shape[:-1] + (-1, 32))
    amax = np.abs(blocks).max(-1, keepdims=True)
    byte = np.maximum(np.where(amax > 0, np.frexp(amax)[1] - 1 + 127, 0) - down, 1)
    scale = np.exp2(byte - 127.0)
    codes = (blocks / scale).astype(np.float32).astype(dtype).astype(np.float64)
    return np.moveaxis((codes * scale).reshape(v.shape), -1, axis)


WIDE = False


def mx_kscale(k):
    if not WIDE:
        return np.ones(k)
    levels = np.array([10, -10, 5, -5, 0])
    a = np.random.permutation(np.resize(levels, k // 512 * 4)).reshape(k // 512, 4)
    idx = np.arange(k)
    return np.exp2(a[idx // 512, idx % 128 // 32])


BF16 = ml_dtypes.bfloat16


def bf(x):
    return np.asarray(x, np.float32).astype(BF16)


def f64(x):
    return np.asarray(x).astype(np.float64)


N, C, F, H, W, KH, KW = 256, 512, 128, 8, 8, 3, 3
P = H * W


def setup_inputs():
    s = mx_kscale(C)[None, :, None, None]
    return {"x_dct": bf(np.random.standard_normal((N, C, H, W)) * 2.0 * s),
            "k_dct": bf(np.random.standard_normal((F, C, H, W)) * 2.0 / np.sqrt(C) / s)}


def reference(x_dct, k_dct):
    xq = mxq(f64(x_dct), 1, "e4m3").reshape(N, C, P).transpose(2, 0, 1)
    kq = mxq(f64(k_dct), 1, "e4m3").reshape(F, C, P).transpose(2, 1, 0)
    r = xq @ kq
    return r.transpose(1, 2, 0).reshape(N, F, H, W)

@@ -1,0 +1,118 @@
+from contextlib import ExitStack
+
+import concourse.mybir as mybir
+from concourse.masks import make_identity
+
+F32 = mybir.dt.float32
+BF16 = mybir.dt.bfloat16
+U32 = mybir.dt.uint32
+U8 = mybir.dt.uint8
+FP8X4 = mybir.dt.float8_e4m3fn_x4
+
+N_IMG, CH, FILT, FREQ = 256, 512, 128, 64
+P = 128
+PACK = 4
+SEG = CH // PACK
+ROWS_PER_TILE = P // PACK
+TILES_PER_UNIT = 4
+BANKS = 8
+FREQ_PER_BANK = FREQ // BANKS
+
+FLOPS = 2 * N_IMG * FILT * CH * FREQ
+
+
+def tile_convdct_pa_kernel(tc, x_dct, k_dct, out):
+    nc = tc.nc
+    x_rows = x_dct.rearrange("n (t q) h w -> (n t) (q h w)", t=PACK)
+    k_rows = k_dct.rearrange("n (t q) h w -> (n t) (q h w)", t=PACK)
+    out_rows = out.rearrange("n f h w -> n (f h w)")
+
+    with ExitStack() as ctx:
+        const = ctx.enter_context(tc.tile_pool(name="const", bufs=1))
+        rawp = ctx.enter_context(tc.tile_pool(name="rawp", bufs=3))
+        grp = ctx.enter_context(tc.tile_pool(name="grp", bufs=12))
+        keep = ctx.enter_context(tc.tile_pool(name="keep", bufs=1))
+        xq = ctx.enter_context(tc.tile_pool(name="xq", bufs=3))
+        outp = ctx.enter_context(tc.tile_pool(name="outp", bufs=1))
+        tps = ctx.enter_context(tc.psum_pool(name="tps", bufs=5))
+        mps = ctx.enter_context(tc.psum_pool(name="mps", bufs=3))
+
+        ident = const.tile([P, P], F32, name="ident")
+        make_identity(nc, ident[:])
+
+        k_codes = keep.tile([P, FREQ * FILT], U32, name="k_codes", align_bytes=64)
+        k_scales = keep.tile([P, FREQ * FILT], U8, name="k_scales", align_bytes=64)
+
+        units = [(k_rows, 0), (x_rows, 0), (x_rows, 1)]
+        for u, (rows, half) in enumerate(units):
+            is_k = u == 0
+            grouped = []
+            out_sb = None
+            if not is_k:
+                out_sb = outp.tile([P, FILT, FREQ], F32, name="out_sb", tag="out_sb")
+            for i in range(TILES_PER_UNIT):
+                raw = rawp.tile([P, SEG * FREQ], BF16, name="raw", tag="raw")
+                r0 = (half * TILES_PER_UNIT + i) * P
+                nc.sync.dma_start(out=raw[:], in_=rows[r0 : r0 + P, :])
+                words = raw[:].bitcast(F32).rearrange("r (q w) -> r q w", w=FREQ // 2)
+                for b in range(BANKS):
+                    bank = tps.tile([P, 512], F32, name="bank", tag="bank")
+                    for j in range(4):
+                        nc.tensor.transpose(
+                            bank[:, j * P : (j + 1) * P], words[:, :, 4 * b + j], ident[:]
+                        )
+                    if i == 0:
+                        g_new = grp.tile(
+                            [P, FREQ_PER_BANK, PACK * P], BF16, name="g", tag="g", align_bytes=64
+                        )
+                        grouped.append(g_new)
+                    dst = grouped[b][:, :, i * P : (i + 1) * P].rearrange(
+                        "q (j e) r -> q j e r", e=2
+                    )
+                    src = bank[:].bitcast(BF16).rearrange("q (j r e) -> q j e r", j=4, e=2)
+                    on_scalar = (b % 2 == 0) or (is_k and i == TILES_PER_UNIT - 1)
+                    if on_scalar:
+                        nc.scalar.copy(out=dst, in_=src)
+                    else:
+                        nc.vector.tensor_copy(out=dst, in_=src)
+            for b in range(BANKS):
+                cols = slice(b * FREQ_PER_BANK * P, (b + 1) * FREQ_PER_BANK * P)
+                flat = grouped[b][:].rearrange("q p r -> q (p r)")
+                if is_k:
+                    nc.vector.quantize_mx(
+                        out=k_codes[:, cols].bitcast(FP8X4), scales=k_scales[:, cols], in_=flat
+                    )
+                    continue
+                x_codes = xq.tile([P, FREQ_PER_BANK * P], U32, name="x_codes", tag="xc", align_bytes=64)
+                x_scales = xq.tile([P, FREQ_PER_BANK * P], U8, name="x_scales", tag="xs", align_bytes=64)
+                nc.vector.quantize_mx(
+                    out=x_codes[:].bitcast(FP8X4), scales=x_scales[:], in_=flat
+                )
+                for h in range(2):
+                    acc = mps.tile([P, 512], F32, name="acc", tag="acc")
+                    for g in range(4):
+                        pl = 4 * h + g
+                        p = FREQ_PER_BANK * b + pl
+                        nc.tensor.matmul_mx(
+                            out=acc[:, g * P : (g + 1) * P],
+                            lhsT=x_codes[:, pl * P : (pl + 1) * P].bitcast(FP8X4),
+                            lhsT_scale=x_scales[:, pl * P : (pl + 1) * P],
+                            rhs=k_codes[:, p * P : (p + 1) * P].bitcast(FP8X4),
+                            rhs_scale=k_scales[:, p * P : (p + 1) * P],
+                            start=True,
+                            stop=True,
+                        )
+                    p0 = FREQ_PER_BANK * b + 4 * h
+                    nc.scalar.copy(
+                        out=out_sb[:, :, p0 : p0 + 4],
+                        in_=acc[:].rearrange("n (g f) -> n f g", g=4),
+                    )
+            if not is_k:
+                n0 = half * P
+                flat_out = out_sb[:].rearrange("n f p -> n (f p)")
+                half_w = FILT * FREQ // 2
+                for s in range(2):
+                    nc.sync.dma_start(
+                        out=out_rows[n0 : n0 + P, s * half_w : (s + 1) * half_w],
+                        in_=flat_out[:, s * half_w : (s + 1) * half_w],
+                    )

@@ -13,12 +13,54 @@ N_IMG, CH, FILT, FREQ = 256, 512, 128, 64
 P = 128
 PACK = 4
 SEG = CH // PACK
-ROWS_PER_TILE = P // PACK
 TILES_PER_UNIT = 4
 BANKS = 8
 FREQ_PER_BANK = FREQ // BANKS
 
 FLOPS = 2 * N_IMG * FILT * CH * FREQ
+
+ORDER = (
+    (0, 0, 0, 0), (0, 1, 0, 0), (1, 0, 0, 0), (1, 0, 1, 0), (2, 0, 0, 0), (1, 0, 2, 0), (2, 0, 1, 1), (1, 0, 3, 0),
+    (1, 0, 4, 0), (2, 0, 3, 0), (3, 0, 2, 1), (1, 0, 5, 0), (2, 0, 4, 1), (4, 0, 2, 0), (0, 2, 0, 0), (1, 0, 6, 0),
+    (1, 0, 7, 0), (2, 0, 6, 0), (3, 0, 5, 1), (1, 1, 0, 0), (2, 0, 7, 1), (4, 0, 5, 0), (1, 1, 1, 0), (2, 1, 0, 0),
+    (1, 1, 2, 0), (2, 1, 1, 1), (1, 1, 3, 0), (1, 1, 4, 0), (2, 1, 3, 0), (3, 1, 2, 1), (1, 1, 5, 0), (2, 1, 4, 1),
+    (4, 1, 2, 0), (0, 3, 0, 0), (1, 1, 6, 0), (1, 1, 7, 0), (2, 1, 6, 0), (3, 1, 5, 1), (1, 2, 0, 0), (2, 1, 7, 1),
+    (4, 1, 5, 0), (1, 2, 1, 0), (2, 2, 0, 0), (1, 2, 2, 0), (2, 2, 1, 1), (1, 2, 3, 0), (1, 2, 4, 0), (2, 2, 3, 0),
+    (3, 2, 2, 1), (1, 2, 5, 0), (2, 2, 4, 1), (4, 2, 2, 0), (0, 4, 0, 0), (1, 2, 6, 0), (1, 2, 7, 0), (2, 2, 6, 0),
+    (3, 2, 5, 1), (1, 3, 0, 0), (2, 2, 7, 1), (4, 2, 5, 0), (1, 3, 1, 0), (2, 3, 0, 0), (1, 3, 2, 0), (2, 3, 1, 1),
+    (1, 3, 3, 0), (5, 0, 0, 0), (1, 3, 4, 0), (3, 3, 2, 1), (1, 3, 5, 0), (2, 3, 3, 0), (2, 3, 4, 1), (4, 3, 2, 0),
+    (0, 5, 0, 0), (1, 3, 6, 0), (1, 3, 7, 0), (2, 3, 6, 0), (3, 3, 5, 1), (1, 4, 0, 0), (2, 3, 7, 1), (4, 3, 5, 0),
+    (1, 4, 1, 0), (2, 4, 0, 0), (1, 4, 2, 0), (2, 4, 1, 1), (1, 4, 3, 0), (5, 0, 1, 0), (1, 4, 4, 0), (3, 4, 2, 1),
+    (1, 4, 5, 0), (0, 6, 0, 0), (2, 4, 3, 1), (5, 0, 2, 0), (1, 4, 6, 0), (1, 4, 7, 0), (2, 4, 4, 1), (5, 0, 3, 0),
+    (1, 5, 0, 0), (1, 5, 1, 0), (3, 4, 5, 1), (5, 0, 4, 0), (1, 5, 2, 0), (2, 4, 6, 1), (5, 0, 5, 0), (1, 5, 3, 0),
+    (2, 4, 7, 1), (0, 7, 0, 0), (1, 5, 4, 0), (5, 0, 6, 0), (2, 5, 0, 1), (1, 5, 5, 0), (2, 5, 1, 1), (5, 0, 7, 0),
+    (1, 5, 6, 0), (3, 5, 2, 1), (2, 5, 3, 0), (4, 4, 2, 0), (1, 5, 7, 0), (2, 5, 4, 1), (1, 6, 0, 0), (2, 5, 6, 0),
+    (0, 8, 0, 0), (4, 4, 5, 0), (3, 5, 5, 1), (1, 6, 1, 0), (2, 5, 7, 1), (1, 6, 2, 0), (2, 6, 0, 0), (1, 6, 3, 0),
+    (4, 5, 2, 0), (2, 6, 1, 1), (1, 6, 4, 0), (2, 6, 3, 0), (1, 6, 5, 0), (4, 5, 5, 0), (3, 6, 2, 1), (1, 6, 6, 0),
+    (2, 6, 4, 0), (3, 6, 5, 1), (1, 6, 7, 0), (2, 6, 6, 1), (1, 7, 0, 0), (0, 9, 0, 0), (2, 6, 7, 0), (4, 6, 2, 0),
+    (1, 7, 1, 0), (2, 7, 0, 1), (1, 7, 2, 0), (2, 7, 1, 0), (4, 6, 5, 0), (1, 7, 3, 0), (3, 7, 2, 1), (1, 7, 4, 0),
+    (2, 7, 3, 0), (1, 7, 5, 0), (2, 7, 4, 1), (4, 7, 2, 0), (1, 7, 6, 0), (1, 7, 7, 0), (2, 7, 6, 0), (3, 7, 5, 1),
+    (1, 8, 0, 0), (2, 7, 7, 1), (4, 7, 5, 0), (0, 10, 0, 0), (1, 8, 1, 0), (2, 8, 0, 0), (1, 8, 2, 0), (2, 8, 1, 1),
+    (1, 8, 3, 0), (5, 1, 0, 0), (1, 8, 4, 0), (3, 8, 2, 1), (1, 8, 5, 0), (5, 1, 1, 0), (2, 8, 3, 1), (6, 1, 0, 0),
+    (6, 1, 0, 1), (1, 8, 6, 0), (7, 1, 0, 1), (5, 1, 2, 0), (6, 1, 1, 0), (7, 1, 1, 1), (6, 1, 1, 1), (7, 1, 2, 1),
+    (1, 8, 7, 0), (5, 1, 3, 0), (7, 1, 3, 1), (0, 11, 0, 0), (6, 1, 2, 0), (6, 1, 2, 1), (7, 1, 4, 1), (1, 9, 0, 0),
+    (5, 1, 4, 0), (7, 1, 5, 1), (6, 1, 3, 0), (6, 1, 3, 1), (7, 1, 6, 1), (6, 1, 4, 0), (5, 1, 5, 0), (7, 1, 7, 1),
+    (6, 1, 4, 1), (7, 1, 8, 1), (6, 1, 5, 0), (5, 1, 6, 0), (7, 1, 9, 1), (6, 1, 5, 1), (7, 1, 10, 1), (7, 1, 11, 1),
+    (6, 1, 6, 0), (5, 1, 7, 0), (6, 1, 6, 1), (7, 1, 12, 1), (7, 1, 13, 1), (6, 1, 7, 0), (2, 8, 4, 0), (4, 8, 2, 0),
+    (6, 1, 7, 1), (7, 1, 14, 1), (7, 1, 15, 1), (1, 9, 1, 0), (2, 8, 6, 0), (8, 1, 0, 0), (3, 8, 5, 1), (1, 9, 2, 0),
+    (2, 8, 7, 1), (4, 8, 5, 0), (2, 9, 0, 0), (1, 9, 3, 0), (1, 9, 4, 0), (2, 9, 1, 1), (2, 9, 3, 0), (1, 9, 5, 0),
+    (1, 9, 6, 0), (3, 9, 2, 1), (2, 9, 4, 0), (1, 9, 7, 0), (3, 9, 5, 1), (4, 9, 2, 0), (1, 10, 0, 0), (2, 9, 6, 1),
+    (2, 9, 7, 0), (1, 10, 1, 0), (4, 9, 5, 0), (1, 10, 2, 0), (2, 10, 0, 1), (2, 10, 1, 0), (1, 10, 3, 0), (1, 10, 4, 0),
+    (3, 10, 2, 1), (2, 10, 3, 0), (1, 10, 5, 0), (2, 10, 4, 1), (4, 10, 2, 0), (1, 10, 6, 0), (1, 10, 7, 0), (2, 10, 6, 0),
+    (3, 10, 5, 1), (1, 11, 0, 0), (2, 10, 7, 1), (4, 10, 5, 0), (1, 11, 1, 0), (2, 11, 0, 0), (1, 11, 2, 0), (2, 11, 1, 1),
+    (1, 11, 3, 0), (5, 2, 0, 0), (1, 11, 4, 0), (3, 11, 2, 1), (1, 11, 5, 0), (2, 11, 3, 1), (2, 11, 4, 0), (4, 11, 2, 0),
+    (1, 11, 6, 0), (1, 11, 7, 0), (3, 11, 5, 1), (2, 11, 6, 0), (6, 2, 0, 0), (2, 11, 7, 1), (4, 11, 5, 0), (6, 2, 0, 1),
+    (7, 2, 0, 1), (5, 2, 1, 0), (7, 2, 1, 1), (6, 2, 1, 0), (5, 2, 2, 0), (6, 2, 1, 1), (7, 2, 2, 1), (7, 2, 3, 1),
+    (6, 2, 2, 0), (5, 2, 3, 0), (6, 2, 2, 1), (7, 2, 4, 1), (7, 2, 5, 1), (6, 2, 3, 0), (5, 2, 4, 0), (6, 2, 3, 1),
+    (7, 2, 6, 1), (7, 2, 7, 1), (6, 2, 4, 0), (5, 2, 5, 0), (6, 2, 4, 1), (7, 2, 8, 1), (7, 2, 9, 1), (6, 2, 5, 0),
+    (5, 2, 6, 0), (6, 2, 5, 1), (7, 2, 10, 1), (7, 2, 11, 1), (6, 2, 6, 0), (5, 2, 7, 0), (6, 2, 6, 1), (7, 2, 12, 1),
+    (7, 2, 13, 1), (6, 2, 7, 0), (6, 2, 7, 1), (7, 2, 14, 1), (7, 2, 15, 1), (8, 2, 0, 0),
+)
 
 
 def tile_convdct_pa_kernel(tc, x_dct, k_dct, out):
@@ -30,7 +72,8 @@ def tile_convdct_pa_kernel(tc, x_dct, k_dct, out):
     with ExitStack() as ctx:
         const = ctx.enter_context(tc.tile_pool(name="const", bufs=1))
         rawp = ctx.enter_context(tc.tile_pool(name="rawp", bufs=3))
-        grp = ctx.enter_context(tc.tile_pool(name="grp", bufs=12))
+        grp = ctx.enter_context(tc.tile_pool(name="grp", bufs=10))
+        hp = ctx.enter_context(tc.tile_pool(name="hp", bufs=3))
         keep = ctx.enter_context(tc.tile_pool(name="keep", bufs=1))
         xq = ctx.enter_context(tc.tile_pool(name="xq", bufs=3))
         outp = ctx.enter_context(tc.tile_pool(name="outp", bufs=1))
@@ -39,77 +82,103 @@ def tile_convdct_pa_kernel(tc, x_dct, k_dct, out):
 
         ident = const.tile([P, P], F32, name="ident")
         make_identity(nc, ident[:])
-
         k_codes = keep.tile([P, FREQ * FILT], U32, name="k_codes", align_bytes=64)
         k_scales = keep.tile([P, FREQ * FILT], U8, name="k_scales", align_bytes=64)
 
-        units = [(k_rows, 0), (x_rows, 0), (x_rows, 1)]
-        for u, (rows, half) in enumerate(units):
-            is_k = u == 0
-            grouped = []
-            out_sb = None
-            if not is_k:
-                out_sb = outp.tile([P, FILT, FREQ], F32, name="out_sb", tag="out_sb")
-            for i in range(TILES_PER_UNIT):
-                raw = rawp.tile([P, SEG * FREQ], BF16, name="raw", tag="raw")
-                r0 = (half * TILES_PER_UNIT + i) * P
-                nc.sync.dma_start(out=raw[:], in_=rows[r0 : r0 + P, :])
-                words = raw[:].bitcast(F32).rearrange("r (q w) -> r q w", w=FREQ // 2)
-                for b in range(BANKS):
-                    bank = tps.tile([P, 512], F32, name="bank", tag="bank")
-                    for j in range(4):
-                        nc.tensor.transpose(
-                            bank[:, j * P : (j + 1) * P], words[:, :, 4 * b + j], ident[:]
-                        )
-                    if i == 0:
-                        g_new = grp.tile(
-                            [P, FREQ_PER_BANK, PACK * P], BF16, name="g", tag="g", align_bytes=64
-                        )
-                        grouped.append(g_new)
-                    dst = grouped[b][:, :, i * P : (i + 1) * P].rearrange(
-                        "q (j e) r -> q j e r", e=2
+        raws = {}
+        banks = {}
+        helds = {}
+        groups = {}
+        codes = {}
+        accs = {}
+        outs = {}
+
+        def group_dst(i, b):
+            u = i // TILES_PER_UNIT
+            if (u, b) not in groups:
+                groups[(u, b)] = grp.tile(
+                    [P, FREQ_PER_BANK, PACK * P], BF16, name="g", tag="g", align_bytes=64
+                )
+            j = i % TILES_PER_UNIT
+            return groups[(u, b)][:, :, j * P : (j + 1) * P].rearrange("q (j e) r -> q j e r", e=2)
+
+        def split_view(words):
+            return words.bitcast(BF16).rearrange("q (j r e) -> q j e r", j=4, e=2)
+
+        ctx.enter_context(tc.manual_schedule())
+        for kind, a, b, c in ORDER:
+            if kind == 0:
+                raws[a] = rawp.tile([P, SEG * FREQ], BF16, name="raw", tag="raw")
+                rows = k_rows if a < TILES_PER_UNIT else x_rows
+                r0 = (a % TILES_PER_UNIT if a < TILES_PER_UNIT else a - TILES_PER_UNIT) * P
+                nc.sync.dma_start(out=raws[a][:], in_=rows[r0 : r0 + P, :])
+            elif kind == 1:
+                words = raws[a][:].bitcast(F32).rearrange("r (q w) -> r q w", w=FREQ // 2)
+                banks[(a, b)] = tps.tile([P, 512], F32, name="bank", tag="bank")
+                for j in range(4):
+                    nc.tensor.transpose(
+                        banks[(a, b)][:, j * P : (j + 1) * P], words[:, :, 4 * b + j], ident[:]
                     )
-                    src = bank[:].bitcast(BF16).rearrange("q (j r e) -> q j e r", j=4, e=2)
-                    on_scalar = (b % 2 == 0) or (is_k and i == TILES_PER_UNIT - 1)
-                    if on_scalar:
-                        nc.scalar.copy(out=dst, in_=src)
-                    else:
-                        nc.vector.tensor_copy(out=dst, in_=src)
-            for b in range(BANKS):
-                cols = slice(b * FREQ_PER_BANK * P, (b + 1) * FREQ_PER_BANK * P)
-                flat = grouped[b][:].rearrange("q p r -> q (p r)")
-                if is_k:
+            elif kind == 2:
+                if c == 0:
+                    nc.vector.tensor_copy(out=group_dst(a, b), in_=split_view(banks[(a, b)][:]))
+                else:
+                    nc.scalar.copy(out=group_dst(a, b), in_=split_view(banks[(a, b)][:]))
+            elif kind == 3:
+                helds[(a, b)] = hp.tile([P, 512], F32, name="held", tag="held")
+                if c == 0:
+                    nc.vector.tensor_copy(out=helds[(a, b)][:], in_=banks[(a, b)][:])
+                else:
+                    nc.scalar.copy(out=helds[(a, b)][:], in_=banks[(a, b)][:])
+            elif kind == 4:
+                nc.gpsimd.tensor_scalar(
+                    out=group_dst(a, b),
+                    in0=split_view(helds[(a, b)][:]),
+                    scalar1=1.0,
+                    scalar2=0.0,
+                    op0=mybir.AluOpType.mult,
+                    op1=mybir.AluOpType.add,
+                )
+            elif kind == 5:
+                flat = groups[(a, b)][:].rearrange("q p r -> q (p r)")
+                if a == 0:
+                    cols = slice(b * FREQ_PER_BANK * P, (b + 1) * FREQ_PER_BANK * P)
                     nc.vector.quantize_mx(
                         out=k_codes[:, cols].bitcast(FP8X4), scales=k_scales[:, cols], in_=flat
                     )
-                    continue
-                x_codes = xq.tile([P, FREQ_PER_BANK * P], U32, name="x_codes", tag="xc", align_bytes=64)
-                x_scales = xq.tile([P, FREQ_PER_BANK * P], U8, name="x_scales", tag="xs", align_bytes=64)
-                nc.vector.quantize_mx(
-                    out=x_codes[:].bitcast(FP8X4), scales=x_scales[:], in_=flat
-                )
-                for h in range(2):
-                    acc = mps.tile([P, 512], F32, name="acc", tag="acc")
-                    for g in range(4):
-                        pl = 4 * h + g
-                        p = FREQ_PER_BANK * b + pl
-                        nc.tensor.matmul_mx(
-                            out=acc[:, g * P : (g + 1) * P],
-                            lhsT=x_codes[:, pl * P : (pl + 1) * P].bitcast(FP8X4),
-                            lhsT_scale=x_scales[:, pl * P : (pl + 1) * P],
-                            rhs=k_codes[:, p * P : (p + 1) * P].bitcast(FP8X4),
-                            rhs_scale=k_scales[:, p * P : (p + 1) * P],
-                            start=True,
-                            stop=True,
-                        )
-                    p0 = FREQ_PER_BANK * b + 4 * h
-                    nc.scalar.copy(
-                        out=out_sb[:, :, p0 : p0 + 4],
-                        in_=acc[:].rearrange("n (g f) -> n f g", g=4),
+                else:
+                    x_codes = xq.tile([P, FREQ_PER_BANK * P], U32, name="x_codes", tag="xc", align_bytes=64)
+                    x_scales = xq.tile([P, FREQ_PER_BANK * P], U8, name="x_scales", tag="xs", align_bytes=64)
+                    codes[(a, b)] = (x_codes, x_scales)
+                    nc.vector.quantize_mx(out=x_codes[:].bitcast(FP8X4), scales=x_scales[:], in_=flat)
+            elif kind == 6:
+                x_codes, x_scales = codes[(a, b)]
+                acc = mps.tile([P, 512], F32, name="acc", tag="acc")
+                accs[(a, 2 * b + c)] = acc
+                for g in range(4):
+                    pl = 4 * c + g
+                    p = FREQ_PER_BANK * b + pl
+                    nc.tensor.matmul_mx(
+                        out=acc[:, g * P : (g + 1) * P],
+                        lhsT=x_codes[:, pl * P : (pl + 1) * P].bitcast(FP8X4),
+                        lhsT_scale=x_scales[:, pl * P : (pl + 1) * P],
+                        rhs=k_codes[:, p * P : (p + 1) * P].bitcast(FP8X4),
+                        rhs_scale=k_scales[:, p * P : (p + 1) * P],
+                        start=True,
+                        stop=True,
                     )
-            if not is_k:
-                n0 = half * P
-                flat_out = out_sb[:].rearrange("n f p -> n (f p)")
+            elif kind == 7:
+                if a not in outs:
+                    outs[a] = outp.tile([P, FILT, FREQ], F32, name="out_sb", tag="out_sb")
+                dst = outs[a][:, :, 4 * b : 4 * b + 4]
+                src = accs[(a, b)][:].rearrange("n (g f) -> n f g", g=4)
+                if c == 0:
+                    nc.vector.tensor_copy(out=dst, in_=src)
+                else:
+                    nc.scalar.copy(out=dst, in_=src)
+            else:
+                n0 = (a - 1) * P
+                flat_out = outs[a][:].rearrange("n f p -> n (f p)")
                 half_w = FILT * FREQ // 2
                 for s in range(2):
                     nc.sync.dma_start(

@@ -13,54 +13,12 @@ N_IMG, CH, FILT, FREQ = 256, 512, 128, 64
 P = 128
 PACK = 4
 SEG = CH // PACK
+ROWS_PER_TILE = P // PACK
 TILES_PER_UNIT = 4
 BANKS = 8
 FREQ_PER_BANK = FREQ // BANKS
 
 FLOPS = 2 * N_IMG * FILT * CH * FREQ
-
-ORDER = (
-    (0, 0, 0, 0), (0, 1, 0, 0), (1, 0, 0, 0), (1, 0, 1, 0), (2, 0, 0, 0), (1, 0, 2, 0), (2, 0, 1, 1), (1, 0, 3, 0),
-    (1, 0, 4, 0), (2, 0, 3, 0), (3, 0, 2, 1), (1, 0, 5, 0), (2, 0, 4, 1), (4, 0, 2, 0), (0, 2, 0, 0), (1, 0, 6, 0),
-    (1, 0, 7, 0), (2, 0, 6, 0), (3, 0, 5, 1), (1, 1, 0, 0), (2, 0, 7, 1), (4, 0, 5, 0), (1, 1, 1, 0), (2, 1, 0, 0),
-    (1, 1, 2, 0), (2, 1, 1, 1), (1, 1, 3, 0), (1, 1, 4, 0), (2, 1, 3, 0), (3, 1, 2, 1), (1, 1, 5, 0), (2, 1, 4, 1),
-    (4, 1, 2, 0), (0, 3, 0, 0), (1, 1, 6, 0), (1, 1, 7, 0), (2, 1, 6, 0), (3, 1, 5, 1), (1, 2, 0, 0), (2, 1, 7, 1),
-    (4, 1, 5, 0), (1, 2, 1, 0), (2, 2, 0, 0), (1, 2, 2, 0), (2, 2, 1, 1), (1, 2, 3, 0), (1, 2, 4, 0), (2, 2, 3, 0),
-    (3, 2, 2, 1), (1, 2, 5, 0), (2, 2, 4, 1), (4, 2, 2, 0), (0, 4, 0, 0), (1, 2, 6, 0), (1, 2, 7, 0), (2, 2, 6, 0),
-    (3, 2, 5, 1), (1, 3, 0, 0), (2, 2, 7, 1), (4, 2, 5, 0), (1, 3, 1, 0), (2, 3, 0, 0), (1, 3, 2, 0), (2, 3, 1, 1),
-    (1, 3, 3, 0), (5, 0, 0, 0), (1, 3, 4, 0), (3, 3, 2, 1), (1, 3, 5, 0), (2, 3, 3, 0), (2, 3, 4, 1), (4, 3, 2, 0),
-    (0, 5, 0, 0), (1, 3, 6, 0), (1, 3, 7, 0), (2, 3, 6, 0), (3, 3, 5, 1), (1, 4, 0, 0), (2, 3, 7, 1), (4, 3, 5, 0),
-    (1, 4, 1, 0), (2, 4, 0, 0), (1, 4, 2, 0), (2, 4, 1, 1), (1, 4, 3, 0), (5, 0, 1, 0), (1, 4, 4, 0), (3, 4, 2, 1),
-    (1, 4, 5, 0), (0, 6, 0, 0), (2, 4, 3, 1), (5, 0, 2, 0), (1, 4, 6, 0), (1, 4, 7, 0), (2, 4, 4, 1), (5, 0, 3, 0),
-    (1, 5, 0, 0), (1, 5, 1, 0), (3, 4, 5, 1), (5, 0, 4, 0), (1, 5, 2, 0), (2, 4, 6, 1), (5, 0, 5, 0), (1, 5, 3, 0),
-    (2, 4, 7, 1), (0, 7, 0, 0), (1, 5, 4, 0), (5, 0, 6, 0), (2, 5, 0, 1), (1, 5, 5, 0), (2, 5, 1, 1), (5, 0, 7, 0),
-    (1, 5, 6, 0), (3, 5, 2, 1), (2, 5, 3, 0), (4, 4, 2, 0), (1, 5, 7, 0), (2, 5, 4, 1), (1, 6, 0, 0), (2, 5, 6, 0),
-    (0, 8, 0, 0), (4, 4, 5, 0), (3, 5, 5, 1), (1, 6, 1, 0), (2, 5, 7, 1), (1, 6, 2, 0), (2, 6, 0, 0), (1, 6, 3, 0),
-    (4, 5, 2, 0), (2, 6, 1, 1), (1, 6, 4, 0), (2, 6, 3, 0), (1, 6, 5, 0), (4, 5, 5, 0), (3, 6, 2, 1), (1, 6, 6, 0),
-    (2, 6, 4, 0), (3, 6, 5, 1), (1, 6, 7, 0), (2, 6, 6, 1), (1, 7, 0, 0), (0, 9, 0, 0), (2, 6, 7, 0), (4, 6, 2, 0),
-    (1, 7, 1, 0), (2, 7, 0, 1), (1, 7, 2, 0), (2, 7, 1, 0), (4, 6, 5, 0), (1, 7, 3, 0), (3, 7, 2, 1), (1, 7, 4, 0),
-    (2, 7, 3, 0), (1, 7, 5, 0), (2, 7, 4, 1), (4, 7, 2, 0), (1, 7, 6, 0), (1, 7, 7, 0), (2, 7, 6, 0), (3, 7, 5, 1),
-    (1, 8, 0, 0), (2, 7, 7, 1), (4, 7, 5, 0), (0, 10, 0, 0), (1, 8, 1, 0), (2, 8, 0, 0), (1, 8, 2, 0), (2, 8, 1, 1),
-    (1, 8, 3, 0), (5, 1, 0, 0), (1, 8, 4, 0), (3, 8, 2, 1), (1, 8, 5, 0), (5, 1, 1, 0), (2, 8, 3, 1), (6, 1, 0, 0),
-    (6, 1, 0, 1), (1, 8, 6, 0), (7, 1, 0, 1), (5, 1, 2, 0), (6, 1, 1, 0), (7, 1, 1, 1), (6, 1, 1, 1), (7, 1, 2, 1),
-    (1, 8, 7, 0), (5, 1, 3, 0), (7, 1, 3, 1), (0, 11, 0, 0), (6, 1, 2, 0), (6, 1, 2, 1), (7, 1, 4, 1), (1, 9, 0, 0),
-    (5, 1, 4, 0), (7, 1, 5, 1), (6, 1, 3, 0), (6, 1, 3, 1), (7, 1, 6, 1), (6, 1, 4, 0), (5, 1, 5, 0), (7, 1, 7, 1),
-    (6, 1, 4, 1), (7, 1, 8, 1), (6, 1, 5, 0), (5, 1, 6, 0), (7, 1, 9, 1), (6, 1, 5, 1), (7, 1, 10, 1), (7, 1, 11, 1),
-    (6, 1, 6, 0), (5, 1, 7, 0), (6, 1, 6, 1), (7, 1, 12, 1), (7, 1, 13, 1), (6, 1, 7, 0), (2, 8, 4, 0), (4, 8, 2, 0),
-    (6, 1, 7, 1), (7, 1, 14, 1), (7, 1, 15, 1), (1, 9, 1, 0), (2, 8, 6, 0), (8, 1, 0, 0), (3, 8, 5, 1), (1, 9, 2, 0),
-    (2, 8, 7, 1), (4, 8, 5, 0), (2, 9, 0, 0), (1, 9, 3, 0), (1, 9, 4, 0), (2, 9, 1, 1), (2, 9, 3, 0), (1, 9, 5, 0),
-    (1, 9, 6, 0), (3, 9, 2, 1), (2, 9, 4, 0), (1, 9, 7, 0), (3, 9, 5, 1), (4, 9, 2, 0), (1, 10, 0, 0), (2, 9, 6, 1),
-    (2, 9, 7, 0), (1, 10, 1, 0), (4, 9, 5, 0), (1, 10, 2, 0), (2, 10, 0, 1), (2, 10, 1, 0), (1, 10, 3, 0), (1, 10, 4, 0),
-    (3, 10, 2, 1), (2, 10, 3, 0), (1, 10, 5, 0), (2, 10, 4, 1), (4, 10, 2, 0), (1, 10, 6, 0), (1, 10, 7, 0), (2, 10, 6, 0),
-    (3, 10, 5, 1), (1, 11, 0, 0), (2, 10, 7, 1), (4, 10, 5, 0), (1, 11, 1, 0), (2, 11, 0, 0), (1, 11, 2, 0), (2, 11, 1, 1),
-    (1, 11, 3, 0), (5, 2, 0, 0), (1, 11, 4, 0), (3, 11, 2, 1), (1, 11, 5, 0), (2, 11, 3, 1), (2, 11, 4, 0), (4, 11, 2, 0),
-    (1, 11, 6, 0), (1, 11, 7, 0), (3, 11, 5, 1), (2, 11, 6, 0), (6, 2, 0, 0), (2, 11, 7, 1), (4, 11, 5, 0), (6, 2, 0, 1),
-    (7, 2, 0, 1), (5, 2, 1, 0), (7, 2, 1, 1), (6, 2, 1, 0), (5, 2, 2, 0), (6, 2, 1, 1), (7, 2, 2, 1), (7, 2, 3, 1),
-    (6, 2, 2, 0), (5, 2, 3, 0), (6, 2, 2, 1), (7, 2, 4, 1), (7, 2, 5, 1), (6, 2, 3, 0), (5, 2, 4, 0), (6, 2, 3, 1),
-    (7, 2, 6, 1), (7, 2, 7, 1), (6, 2, 4, 0), (5, 2, 5, 0), (6, 2, 4, 1), (7, 2, 8, 1), (7, 2, 9, 1), (6, 2, 5, 0),
-    (5, 2, 6, 0), (6, 2, 5, 1), (7, 2, 10, 1), (7, 2, 11, 1), (6, 2, 6, 0), (5, 2, 7, 0), (6, 2, 6, 1), (7, 2, 12, 1),
-    (7, 2, 13, 1), (6, 2, 7, 0), (6, 2, 7, 1), (7, 2, 14, 1), (7, 2, 15, 1), (8, 2, 0, 0),
-)
 
 
 def tile_convdct_pa_kernel(tc, x_dct, k_dct, out):
@@ -72,8 +30,7 @@ def tile_convdct_pa_kernel(tc, x_dct, k_dct, out):
     with ExitStack() as ctx:
         const = ctx.enter_context(tc.tile_pool(name="const", bufs=1))
         rawp = ctx.enter_context(tc.tile_pool(name="rawp", bufs=3))
-        grp = ctx.enter_context(tc.tile_pool(name="grp", bufs=10))
-        hp = ctx.enter_context(tc.tile_pool(name="hp", bufs=3))
+        grp = ctx.enter_context(tc.tile_pool(name="grp", bufs=12))
         keep = ctx.enter_context(tc.tile_pool(name="keep", bufs=1))
         xq = ctx.enter_context(tc.tile_pool(name="xq", bufs=3))
         outp = ctx.enter_context(tc.tile_pool(name="outp", bufs=1))
@@ -82,103 +39,73 @@ def tile_convdct_pa_kernel(tc, x_dct, k_dct, out):
 
         ident = const.tile([P, P], F32, name="ident")
         make_identity(nc, ident[:])
+
         k_codes = keep.tile([P, FREQ * FILT], U32, name="k_codes", align_bytes=64)
         k_scales = keep.tile([P, FREQ * FILT], U8, name="k_scales", align_bytes=64)
 
-        raws = {}
-        banks = {}
-        helds = {}
-        groups = {}
-        codes = {}
-        accs = {}
-        outs = {}
-
-        def group_dst(i, b):
-            u = i // TILES_PER_UNIT
-            if (u, b) not in groups:
-                groups[(u, b)] = grp.tile(
-                    [P, FREQ_PER_BANK, PACK * P], BF16, name="g", tag="g", align_bytes=64
-                )
-            j = i % TILES_PER_UNIT
-            return groups[(u, b)][:, :, j * P : (j + 1) * P].rearrange("q (j e) r -> q j e r", e=2)
-
-        def split_view(words):
-            return words.bitcast(BF16).rearrange("q (j r e) -> q j e r", j=4, e=2)
-
-        ctx.enter_context(tc.manual_schedule())
-        for kind, a, b, c in ORDER:
-            if kind == 0:
-                raws[a] = rawp.tile([P, SEG * FREQ], BF16, name="raw", tag="raw")
-                rows = k_rows if a < TILES_PER_UNIT else x_rows
-                r0 = (a % TILES_PER_UNIT if a < TILES_PER_UNIT else a - TILES_PER_UNIT) * P
-                nc.sync.dma_start(out=raws[a][:], in_=rows[r0 : r0 + P, :])
-            elif kind == 1:
-                words = raws[a][:].bitcast(F32).rearrange("r (q w) -> r q w", w=FREQ // 2)
-                banks[(a, b)] = tps.tile([P, 512], F32, name="bank", tag="bank")
-                for j in range(4):
-                    nc.tensor.transpose(
-                        banks[(a, b)][:, j * P : (j + 1) * P], words[:, :, 4 * b + j], ident[:]
+        units = [(k_rows, 0), (x_rows, 0), (x_rows, 1)]
+        for u, (rows, half) in enumerate(units):
+            is_k = u == 0
+            grouped = []
+            out_sb = None
+            if not is_k:
+                out_sb = outp.tile([P, FILT, FREQ], F32, name="out_sb", tag="out_sb")
+            for i in range(TILES_PER_UNIT):
+                raw = rawp.tile([P, SEG * FREQ], BF16, name="raw", tag="raw")
+                r0 = (half * TILES_PER_UNIT + i) * P
+                nc.sync.dma_start(out=raw[:], in_=rows[r0 : r0 + P, :])
+                words = raw[:].bitcast(F32).rearrange("r (q w) -> r q w", w=FREQ // 2)
+                for b in range(BANKS):
+                    bank = tps.tile([P, 512], F32, name="bank", tag="bank")
+                    for j in range(4):
+                        nc.tensor.transpose(
+                            bank[:, j * P : (j + 1) * P], words[:, :, 4 * b + j], ident[:]
+                        )
+                    if i == 0:
+                        g_new = grp.tile(
+                            [P, FREQ_PER_BANK, PACK * P], BF16, name="g", tag="g", align_bytes=64
+                        )
+                        grouped.append(g_new)
+                    dst = grouped[b][:, :, i * P : (i + 1) * P].rearrange(
+                        "q (j e) r -> q j e r", e=2
                     )
-            elif kind == 2:
-                if c == 0:
-                    nc.vector.tensor_copy(out=group_dst(a, b), in_=split_view(banks[(a, b)][:]))
-                else:
-                    nc.scalar.copy(out=group_dst(a, b), in_=split_view(banks[(a, b)][:]))
-            elif kind == 3:
-                helds[(a, b)] = hp.tile([P, 512], F32, name="held", tag="held")
-                if c == 0:
-                    nc.vector.tensor_copy(out=helds[(a, b)][:], in_=banks[(a, b)][:])
-                else:
-                    nc.scalar.copy(out=helds[(a, b)][:], in_=banks[(a, b)][:])
-            elif kind == 4:
-                nc.gpsimd.tensor_scalar(
-                    out=group_dst(a, b),
-                    in0=split_view(helds[(a, b)][:]),
-                    scalar1=1.0,
-                    scalar2=0.0,
-                    op0=mybir.AluOpType.mult,
-                    op1=mybir.AluOpType.add,
-                )
-            elif kind == 5:
-                flat = groups[(a, b)][:].rearrange("q p r -> q (p r)")
-                if a == 0:
-                    cols = slice(b * FREQ_PER_BANK * P, (b + 1) * FREQ_PER_BANK * P)
+                    src = bank[:].bitcast(BF16).rearrange("q (j r e) -> q j e r", j=4, e=2)
+                    nc.any.tensor_copy(out=dst, in_=src)
+            for b in range(BANKS):
+                cols = slice(b * FREQ_PER_BANK * P, (b + 1) * FREQ_PER_BANK * P)
+                flat = grouped[b][:].rearrange("q p r -> q (p r)")
+                if is_k:
                     nc.vector.quantize_mx(
                         out=k_codes[:, cols].bitcast(FP8X4), scales=k_scales[:, cols], in_=flat
                     )
-                else:
-                    x_codes = xq.tile([P, FREQ_PER_BANK * P], U32, name="x_codes", tag="xc", align_bytes=64)
-                    x_scales = xq.tile([P, FREQ_PER_BANK * P], U8, name="x_scales", tag="xs", align_bytes=64)
-                    codes[(a, b)] = (x_codes, x_scales)
-                    nc.vector.quantize_mx(out=x_codes[:].bitcast(FP8X4), scales=x_scales[:], in_=flat)
-            elif kind == 6:
-                x_codes, x_scales = codes[(a, b)]
-                acc = mps.tile([P, 512], F32, name="acc", tag="acc")
-                accs[(a, 2 * b + c)] = acc
-                for g in range(4):
-                    pl = 4 * c + g
-                    p = FREQ_PER_BANK * b + pl
-                    nc.tensor.matmul_mx(
-                        out=acc[:, g * P : (g + 1) * P],
-                        lhsT=x_codes[:, pl * P : (pl + 1) * P].bitcast(FP8X4),
-                        lhsT_scale=x_scales[:, pl * P : (pl + 1) * P],
-                        rhs=k_codes[:, p * P : (p + 1) * P].bitcast(FP8X4),
-                        rhs_scale=k_scales[:, p * P : (p + 1) * P],
-                        start=True,
-                        stop=True,
+                    continue
+                x_codes = xq.tile([P, FREQ_PER_BANK * P], U32, name="x_codes", tag="xc", align_bytes=64)
+                x_scales = xq.tile([P, FREQ_PER_BANK * P], U8, name="x_scales", tag="xs", align_bytes=64)
+                nc.vector.quantize_mx(
+                    out=x_codes[:].bitcast(FP8X4), scales=x_scales[:], in_=flat
+                )
+                for h in range(2):
+                    acc = mps.tile([P, 512], F32, name="acc", tag="acc")
+                    for g in range(4):
+                        pl = 4 * h + g
+                        p = FREQ_PER_BANK * b + pl
+                        nc.tensor.matmul_mx(
+                            out=acc[:, g * P : (g + 1) * P],
+                            lhsT=x_codes[:, pl * P : (pl + 1) * P].bitcast(FP8X4),
+                            lhsT_scale=x_scales[:, pl * P : (pl + 1) * P],
+                            rhs=k_codes[:, p * P : (p + 1) * P].bitcast(FP8X4),
+                            rhs_scale=k_scales[:, p * P : (p + 1) * P],
+                            start=True,
+                            stop=True,
+                        )
+                    p0 = FREQ_PER_BANK * b + 4 * h
+                    nc.scalar.copy(
+                        out=out_sb[:, :, p0 : p0 + 4],
+                        in_=acc[:].rearrange("n (g f) -> n f g", g=4),
                     )
-            elif kind == 7:
-                if a not in outs:
-                    outs[a] = outp.tile([P, FILT, FREQ], F32, name="out_sb", tag="out_sb")
-                dst = outs[a][:, :, 4 * b : 4 * b + 4]
-                src = accs[(a, b)][:].rearrange("n (g f) -> n f g", g=4)
-                if c == 0:
-                    nc.vector.tensor_copy(out=dst, in_=src)
-                else:
-                    nc.scalar.copy(out=dst, in_=src)
-            else:
-                n0 = (a - 1) * P
-                flat_out = outs[a][:].rearrange("n f p -> n (f p)")
+            if not is_k:
+                n0 = half * P
+                flat_out = out_sb[:].rearrange("n f p -> n (f p)")
                 half_w = FILT * FREQ // 2
                 for s in range(2):
                     nc.sync.dma_start(

@@ -13,10 +13,10 @@ N_IMG, CH, FILT, FREQ = 256, 512, 128, 64
 P = 128
 PACK = 4
 SEG = CH // PACK
-ROWS_PER_TILE = P // PACK
 TILES_PER_UNIT = 4
-BANKS = 8
-FREQ_PER_BANK = FREQ // BANKS
+TILES = 12
+GROUPS = 8
+FREQ_PER_GROUP = FREQ // GROUPS
 
 FLOPS = 2 * N_IMG * FILT * CH * FREQ
 
@@ -29,86 +29,127 @@ def tile_convdct_pa_kernel(tc, x_dct, k_dct, out):
 
     with ExitStack() as ctx:
         const = ctx.enter_context(tc.tile_pool(name="const", bufs=1))
-        rawp = ctx.enter_context(tc.tile_pool(name="rawp", bufs=3))
-        grp = ctx.enter_context(tc.tile_pool(name="grp", bufs=12))
+        rawp = ctx.enter_context(tc.tile_pool(name="rawp", bufs=4))
+        grp = ctx.enter_context(tc.tile_pool(name="grp", bufs=11))
         keep = ctx.enter_context(tc.tile_pool(name="keep", bufs=1))
         xq = ctx.enter_context(tc.tile_pool(name="xq", bufs=3))
         outp = ctx.enter_context(tc.tile_pool(name="outp", bufs=1))
         tps = ctx.enter_context(tc.psum_pool(name="tps", bufs=5))
         mps = ctx.enter_context(tc.psum_pool(name="mps", bufs=3))
 
-        ident = const.tile([P, P], F32, name="ident")
+        ident = const.tile([P, P], BF16, name="ident")
         make_identity(nc, ident[:])
-
         k_codes = keep.tile([P, FREQ * FILT], U32, name="k_codes", align_bytes=64)
         k_scales = keep.tile([P, FREQ * FILT], U8, name="k_scales", align_bytes=64)
 
-        units = [(k_rows, 0), (x_rows, 0), (x_rows, 1)]
-        for u, (rows, half) in enumerate(units):
-            is_k = u == 0
-            grouped = []
-            out_sb = None
-            if not is_k:
-                out_sb = outp.tile([P, FILT, FREQ], F32, name="out_sb", tag="out_sb")
-            for i in range(TILES_PER_UNIT):
-                raw = rawp.tile([P, SEG * FREQ], BF16, name="raw", tag="raw")
-                r0 = (half * TILES_PER_UNIT + i) * P
-                nc.sync.dma_start(out=raw[:], in_=rows[r0 : r0 + P, :])
-                words = raw[:].bitcast(F32).rearrange("r (q w) -> r q w", w=FREQ // 2)
-                for b in range(BANKS):
-                    bank = tps.tile([P, 512], F32, name="bank", tag="bank")
-                    for j in range(4):
-                        nc.tensor.transpose(
-                            bank[:, j * P : (j + 1) * P], words[:, :, 4 * b + j], ident[:]
-                        )
-                    if i == 0:
-                        g_new = grp.tile(
-                            [P, FREQ_PER_BANK, PACK * P], BF16, name="g", tag="g", align_bytes=64
-                        )
-                        grouped.append(g_new)
-                    dst = grouped[b][:, :, i * P : (i + 1) * P].rearrange(
-                        "q (j e) r -> q j e r", e=2
+        raws = {}
+        groups = {}
+        codes = {}
+        outs = {}
+
+        def load(i):
+            raws[i] = rawp.tile([P, SEG * FREQ], BF16, name="raw", tag="raw")
+            rows = k_rows if i < TILES_PER_UNIT else x_rows
+            r0 = (i % TILES_PER_UNIT if i < TILES_PER_UNIT else i - TILES_PER_UNIT) * P
+            nc.sync.dma_start(out=raws[i][:], in_=rows[r0 : r0 + P, :])
+
+        def turn(i, b, engine):
+            u, j = divmod(i, TILES_PER_UNIT)
+            elems = raws[i][:].rearrange("r (q p) -> r q p", p=FREQ)
+            bank = tps.tile([P, FREQ_PER_GROUP, P], BF16, name="bank", tag="bank")
+            for g in range(FREQ_PER_GROUP):
+                nc.tensor.transpose(bank[:, g, :], elems[:, :, FREQ_PER_GROUP * b + g], ident[:])
+            if (u, b) not in groups:
+                groups[(u, b)] = grp.tile([P, FREQ_PER_GROUP, PACK * P], BF16, name="g", tag="g", align_bytes=64)
+            dst = groups[(u, b)][:, :, j * P : (j + 1) * P]
+            if engine == 0:
+                nc.vector.tensor_copy(out=dst, in_=bank[:])
+            else:
+                nc.scalar.copy(out=dst, in_=bank[:])
+
+        def quantise(u, b):
+            flat = groups[(u, b)][:].rearrange("q p r -> q (p r)")
+            if u == 0:
+                cols = slice(b * FREQ_PER_GROUP * P, (b + 1) * FREQ_PER_GROUP * P)
+                nc.vector.quantize_mx(out=k_codes[:, cols].bitcast(FP8X4), scales=k_scales[:, cols], in_=flat)
+            else:
+                x_codes = xq.tile([P, FREQ_PER_GROUP * P], U32, name="x_codes", tag="xc", align_bytes=64)
+                x_scales = xq.tile([P, FREQ_PER_GROUP * P], U8, name="x_scales", tag="xs", align_bytes=64)
+                codes[(u, b)] = (x_codes, x_scales)
+                nc.vector.quantize_mx(out=x_codes[:].bitcast(FP8X4), scales=x_scales[:], in_=flat)
+
+        def multiply(u, b, engines):
+            x_codes, x_scales = codes[(u, b)]
+            accs = []
+            for c in range(2):
+                acc = mps.tile([P, 512], F32, name="acc", tag="acc")
+                accs.append(acc)
+                for g in range(4):
+                    pl = 4 * c + g
+                    p = FREQ_PER_GROUP * b + pl
+                    nc.tensor.matmul_mx(
+                        out=acc[:, g * P : (g + 1) * P],
+                        lhsT=x_codes[:, pl * P : (pl + 1) * P].bitcast(FP8X4),
+                        lhsT_scale=x_scales[:, pl * P : (pl + 1) * P],
+                        rhs=k_codes[:, p * P : (p + 1) * P].bitcast(FP8X4),
+                        rhs_scale=k_scales[:, p * P : (p + 1) * P],
+                        start=True,
+                        stop=True,
                     )
-                    src = bank[:].bitcast(BF16).rearrange("q (j r e) -> q j e r", j=4, e=2)
-                    nc.any.tensor_copy(out=dst, in_=src)
-            for b in range(BANKS):
-                cols = slice(b * FREQ_PER_BANK * P, (b + 1) * FREQ_PER_BANK * P)
-                flat = grouped[b][:].rearrange("q p r -> q (p r)")
-                if is_k:
-                    nc.vector.quantize_mx(
-                        out=k_codes[:, cols].bitcast(FP8X4), scales=k_scales[:, cols], in_=flat
-                    )
-                    continue
-                x_codes = xq.tile([P, FREQ_PER_BANK * P], U32, name="x_codes", tag="xc", align_bytes=64)
-                x_scales = xq.tile([P, FREQ_PER_BANK * P], U8, name="x_scales", tag="xs", align_bytes=64)
-                nc.vector.quantize_mx(
-                    out=x_codes[:].bitcast(FP8X4), scales=x_scales[:], in_=flat
-                )
-                for h in range(2):
-                    acc = mps.tile([P, 512], F32, name="acc", tag="acc")
-                    for g in range(4):
-                        pl = 4 * h + g
-                        p = FREQ_PER_BANK * b + pl
-                        nc.tensor.matmul_mx(
-                            out=acc[:, g * P : (g + 1) * P],
-                            lhsT=x_codes[:, pl * P : (pl + 1) * P].bitcast(FP8X4),
-                            lhsT_scale=x_scales[:, pl * P : (pl + 1) * P],
-                            rhs=k_codes[:, p * P : (p + 1) * P].bitcast(FP8X4),
-                            rhs_scale=k_scales[:, p * P : (p + 1) * P],
-                            start=True,
-                            stop=True,
-                        )
-                    p0 = FREQ_PER_BANK * b + 4 * h
-                    nc.scalar.copy(
-                        out=out_sb[:, :, p0 : p0 + 4],
-                        in_=acc[:].rearrange("n (g f) -> n f g", g=4),
-                    )
-            if not is_k:
-                n0 = half * P
-                flat_out = out_sb[:].rearrange("n f p -> n (f p)")
-                half_w = FILT * FREQ // 2
-                for s in range(2):
-                    nc.sync.dma_start(
-                        out=out_rows[n0 : n0 + P, s * half_w : (s + 1) * half_w],
-                        in_=flat_out[:, s * half_w : (s + 1) * half_w],
-                    )
+            if b == 0:
+                if u == 1:
+                    outs[u] = [outp.tile([P, FILT, FREQ], F32, name="out_sb", tag="out_sb")]
+                else:
+                    outs[u] = [rawp.tile([P, FILT // 2, FREQ], F32, name="out_h", tag="raw") for h in range(2)]
+            parts = outs[u]
+            width = FILT // len(parts)
+            for c in range(2):
+                for h in range(len(parts)):
+                    p0 = FREQ_PER_GROUP * b + 4 * c
+                    dst = parts[h][:, :, p0 : p0 + 4]
+                    src = accs[c][:].rearrange("n (g f) -> n f g", g=4)[:, h * width : (h + 1) * width, :]
+                    if engines[c] == 0:
+                        nc.vector.tensor_copy(out=dst, in_=src)
+                    else:
+                        nc.scalar.copy(out=dst, in_=src)
+
+        def store(u):
+            n0 = (u - 1) * P
+            parts = outs[u]
+            half = FILT * FREQ // 2
+            for s in range(2):
+                if len(parts) == 1:
+                    src = parts[0][:].rearrange("n f p -> n (f p)")[:, s * half : (s + 1) * half]
+                else:
+                    src = parts[s][:].rearrange("n f p -> n (f p)")
+                nc.sync.dma_start(out=out_rows[n0 : n0 + P, s * half : (s + 1) * half], in_=src)
+
+        steps = [(i, b) for i in range(10) for b in range(GROUPS)]
+        steps += [(i, b) for b in range(GROUPS) for i in (10, 11)]
+        at = {}
+        for b in range(GROUPS):
+            at.setdefault(25 + 3 * b, []).append((quantise, (0, b)))
+            at.setdefault(57 + 3 * b, []).append((quantise, (1, b)))
+            at.setdefault(61 + 3 * b, []).append((multiply, (1, b, (1, 1))))
+            at.setdefault(82 + 2 * b, []).append((quantise, (2, b)))
+            at.setdefault(85 + 2 * b, []).append((multiply, (2, b, (1, 1) if b < 7 else (0, 1))))
+        at.setdefault(82, []).append((store, (1,)))
+        at[101] = [(store, (2,))]
+
+        ctx.enter_context(tc.manual_schedule())
+        for i in range(4):
+            load(i)
+        for s in range(102):
+            if s % GROUPS == 0 and s > 0 and s // GROUPS + 4 - 1 < TILES:
+                load(s // GROUPS + 4 - 1)
+            if s < len(steps):
+                i, b = steps[s]
+                if 25 <= s < 49:
+                    engine = 0 if s % 4 == 3 else 1
+                elif s >= 80:
+                    engine = s % 2
+                else:
+                    engine = s % 2
+                turn(i, b, engine)
+            for act, args in at.get(s, []):
+                act(*args)

@@ -15,8 +15,13 @@ PACK = 4
 SEG = CH // PACK
 TILES_PER_UNIT = 4
 TILES = 12
+TURNED = TILES - 1
 GROUPS = 8
 FREQ_PER_GROUP = FREQ // GROUPS
+WORDS = FREQ // 2
+WORDS_PER_GROUP = WORDS // GROUPS
+HALF = P // 2
+ROW_BYTES = SEG * FREQ * 2
 
 FLOPS = 2 * N_IMG * FILT * CH * FREQ
 
@@ -25,19 +30,20 @@ def tile_convdct_pa_kernel(tc, x_dct, k_dct, out):
     nc = tc.nc
     x_rows = x_dct.rearrange("n (t q) h w -> (n t) (q h w)", t=PACK)
     k_rows = k_dct.rearrange("n (t q) h w -> (n t) (q h w)", t=PACK)
+    x_channels = x_dct.rearrange("n (t q) h w -> q (n t) (h w)", t=PACK)
     out_rows = out.rearrange("n f h w -> n (f h w)")
 
     with ExitStack() as ctx:
         const = ctx.enter_context(tc.tile_pool(name="const", bufs=1))
-        rawp = ctx.enter_context(tc.tile_pool(name="rawp", bufs=4))
-        grp = ctx.enter_context(tc.tile_pool(name="grp", bufs=11))
+        rawp = ctx.enter_context(tc.tile_pool(name="rawp", bufs=3))
+        grp = ctx.enter_context(tc.tile_pool(name="grp", bufs=10))
         keep = ctx.enter_context(tc.tile_pool(name="keep", bufs=1))
         xq = ctx.enter_context(tc.tile_pool(name="xq", bufs=3))
         outp = ctx.enter_context(tc.tile_pool(name="outp", bufs=1))
         tps = ctx.enter_context(tc.psum_pool(name="tps", bufs=5))
         mps = ctx.enter_context(tc.psum_pool(name="mps", bufs=3))
 
-        ident = const.tile([P, P], BF16, name="ident")
+        ident = const.tile([P, P], F32, name="ident")
         make_identity(nc, ident[:])
         k_codes = keep.tile([P, FREQ * FILT], U32, name="k_codes", align_bytes=64)
         k_scales = keep.tile([P, FREQ * FILT], U8, name="k_scales", align_bytes=64)
@@ -46,28 +52,60 @@ def tile_convdct_pa_kernel(tc, x_dct, k_dct, out):
         groups = {}
         codes = {}
         outs = {}
+        given = {"V": 0, "S": 0}
+
+        def lighter(columns):
+            engine = "V" if given["V"] <= given["S"] else "S"
+            given[engine] += columns
+            return engine
+
+        def copy(engine, dst, src):
+            if engine == "V":
+                nc.vector.tensor_copy(out=dst, in_=src)
+            else:
+                nc.scalar.copy(out=dst, in_=src)
 
         def load(i):
-            raws[i] = rawp.tile([P, SEG * FREQ], BF16, name="raw", tag="raw")
+            slot = i % 3
+            raws[i] = rawp.tile([P, SEG * FREQ], BF16, name="raw", tag="raw%d" % slot, offset=slot * ROW_BYTES, bufs=1)
             rows = k_rows if i < TILES_PER_UNIT else x_rows
             r0 = (i % TILES_PER_UNIT if i < TILES_PER_UNIT else i - TILES_PER_UNIT) * P
             nc.sync.dma_start(out=raws[i][:], in_=rows[r0 : r0 + P, :])
 
-        def turn(i, b, engine):
-            u, j = divmod(i, TILES_PER_UNIT)
-            elems = raws[i][:].rearrange("r (q p) -> r q p", p=FREQ)
-            bank = tps.tile([P, FREQ_PER_GROUP, P], BF16, name="bank", tag="bank")
-            for g in range(FREQ_PER_GROUP):
-                nc.tensor.transpose(bank[:, g, :], elems[:, :, FREQ_PER_GROUP * b + g], ident[:])
+        def load_direct(h):
+            if h == 0:
+                raws[TURNED] = rawp.tile([P, P, FREQ], BF16, name="direct", tag="direct", offset=3 * ROW_BYTES, bufs=1)
+            r0 = (TURNED - TILES_PER_UNIT) * P + h * HALF
+            nc.sync.dma_start(
+                out=raws[TURNED][:, h * HALF : (h + 1) * HALF, :], in_=x_channels[:, r0 : r0 + HALF, :]
+            )
+
+        def group_dst(u, b, c0, c1):
             if (u, b) not in groups:
                 groups[(u, b)] = grp.tile([P, FREQ_PER_GROUP, PACK * P], BF16, name="g", tag="g", align_bytes=64)
-            dst = groups[(u, b)][:, :, j * P : (j + 1) * P]
-            if engine == 0:
-                nc.vector.tensor_copy(out=dst, in_=bank[:])
-            else:
-                nc.scalar.copy(out=dst, in_=bank[:])
+            return groups[(u, b)][:, :, c0:c1]
+
+        def turn(i, b):
+            u, j = divmod(i, TILES_PER_UNIT)
+            words = raws[i][:].bitcast(F32).rearrange("r (q w) -> r w q", w=WORDS)
+            bank = tps.tile([P, WORDS_PER_GROUP * P], F32, name="bank", tag="bank")
+            for g in range(WORDS_PER_GROUP):
+                nc.tensor.transpose(bank[:, g * P : (g + 1) * P], words[:, WORDS_PER_GROUP * b + g, :], ident[:])
+            dst = group_dst(u, b, j * P, (j + 1) * P).rearrange("q (j e) r -> q j e r", e=2)
+            src = bank[:].bitcast(BF16).rearrange("q (j r e) -> q j e r", j=WORDS_PER_GROUP, e=2)
+            copy(lighter(2 * WORDS_PER_GROUP * P), dst, src)
+
+        def spread(b, h):
+            c0 = (TURNED % TILES_PER_UNIT) * P + h * HALF
+            dst = group_dst(TURNED // TILES_PER_UNIT, b, c0, c0 + HALF).rearrange("q (v i) r -> q v r i", i=4)
+            freqs = slice(FREQ_PER_GROUP * b, FREQ_PER_GROUP * (b + 1))
+            src = raws[TURNED][:, h * HALF : (h + 1) * HALF, freqs].rearrange("q r (v i) -> q v r i", i=4)
+            nc.gpsimd.tensor_scalar(
+                out=dst, in0=src, scalar1=1.0, scalar2=0.0, op0=mybir.AluOpType.mult, op1=mybir.AluOpType.add
+            )
 
         def quantise(u, b):
+            given["V"] += FREQ_PER_GROUP * P
             flat = groups[(u, b)][:].rearrange("q p r -> q (p r)")
             if u == 0:
                 cols = slice(b * FREQ_PER_GROUP * P, (b + 1) * FREQ_PER_GROUP * P)
@@ -78,78 +116,60 @@ def tile_convdct_pa_kernel(tc, x_dct, k_dct, out):
                 codes[(u, b)] = (x_codes, x_scales)
                 nc.vector.quantize_mx(out=x_codes[:].bitcast(FP8X4), scales=x_scales[:], in_=flat)
 
-        def multiply(u, b, engines):
+        def multiply(u, b):
             x_codes, x_scales = codes[(u, b)]
-            accs = []
+            if b == 0:
+                if u == 1:
+                    outs[u] = outp.tile([P, FILT, FREQ], F32, name="out_1", tag="out_1")
+                else:
+                    outs[u] = rawp.tile([P, FILT, FREQ], F32, name="out_2", tag="out_2", offset=2 * ROW_BYTES, bufs=1)
             for c in range(2):
-                acc = mps.tile([P, 512], F32, name="acc", tag="acc")
-                accs.append(acc)
+                acc = mps.tile([P, 4 * FILT], F32, name="acc", tag="acc")
                 for g in range(4):
                     pl = 4 * c + g
                     p = FREQ_PER_GROUP * b + pl
                     nc.tensor.matmul_mx(
-                        out=acc[:, g * P : (g + 1) * P],
+                        out=acc[:, g * FILT : (g + 1) * FILT],
                         lhsT=x_codes[:, pl * P : (pl + 1) * P].bitcast(FP8X4),
                         lhsT_scale=x_scales[:, pl * P : (pl + 1) * P],
-                        rhs=k_codes[:, p * P : (p + 1) * P].bitcast(FP8X4),
-                        rhs_scale=k_scales[:, p * P : (p + 1) * P],
+                        rhs=k_codes[:, p * FILT : (p + 1) * FILT].bitcast(FP8X4),
+                        rhs_scale=k_scales[:, p * FILT : (p + 1) * FILT],
                         start=True,
                         stop=True,
                     )
-            if b == 0:
-                if u == 1:
-                    outs[u] = [outp.tile([P, FILT, FREQ], F32, name="out_sb", tag="out_sb")]
-                else:
-                    outs[u] = [rawp.tile([P, FILT // 2, FREQ], F32, name="out_h", tag="raw") for h in range(2)]
-            parts = outs[u]
-            width = FILT // len(parts)
-            for c in range(2):
-                for h in range(len(parts)):
-                    p0 = FREQ_PER_GROUP * b + 4 * c
-                    dst = parts[h][:, :, p0 : p0 + 4]
-                    src = accs[c][:].rearrange("n (g f) -> n f g", g=4)[:, h * width : (h + 1) * width, :]
-                    if engines[c] == 0:
-                        nc.vector.tensor_copy(out=dst, in_=src)
-                    else:
-                        nc.scalar.copy(out=dst, in_=src)
+                p0 = FREQ_PER_GROUP * b + 4 * c
+                copy(lighter(4 * FILT), outs[u][:, :, p0 : p0 + 4], acc[:].rearrange("n (g f) -> n f g", g=4))
 
         def store(u):
             n0 = (u - 1) * P
-            parts = outs[u]
+            flat = outs[u][:].rearrange("n f p -> n (f p)")
             half = FILT * FREQ // 2
             for s in range(2):
-                if len(parts) == 1:
-                    src = parts[0][:].rearrange("n f p -> n (f p)")[:, s * half : (s + 1) * half]
-                else:
-                    src = parts[s][:].rearrange("n f p -> n (f p)")
-                nc.sync.dma_start(out=out_rows[n0 : n0 + P, s * half : (s + 1) * half], in_=src)
+                nc.sync.dma_start(out=out_rows[n0 : n0 + P, s * half : (s + 1) * half], in_=flat[:, s * half : (s + 1) * half])
 
-        steps = [(i, b) for i in range(10) for b in range(GROUPS)]
-        steps += [(i, b) for b in range(GROUPS) for i in (10, 11)]
         at = {}
         for b in range(GROUPS):
-            at.setdefault(25 + 3 * b, []).append((quantise, (0, b)))
-            at.setdefault(57 + 3 * b, []).append((quantise, (1, b)))
-            at.setdefault(61 + 3 * b, []).append((multiply, (1, b, (1, 1))))
-            at.setdefault(82 + 2 * b, []).append((quantise, (2, b)))
-            at.setdefault(85 + 2 * b, []).append((multiply, (2, b, (1, 1) if b < 7 else (0, 1))))
-        at.setdefault(82, []).append((store, (1,)))
-        at[101] = [(store, (2,))]
+            at.setdefault(25 + (4 * b) // 2, []).append((quantise, (0, b)))
+            at.setdefault(57 + (5 * b) // 2, []).append((quantise, (1, b)))
+            at.setdefault(61 + (5 * b) // 2, []).append((multiply, (1, b)))
+            for h in range(2):
+                at.setdefault(73 + h, []).append((spread, (b, h)))
+            at.setdefault(81 + b, []).append((quantise, (2, b)))
+            at.setdefault(84 + b, []).append((multiply, (2, b)))
+        at.setdefault(84, []).append((store, (1,)))
+        last = max(at)
+        at[last].append((store, (2,)))
 
         ctx.enter_context(tc.manual_schedule())
-        for i in range(4):
+        for i in range(3):
             load(i)
-        for s in range(102):
-            if s % GROUPS == 0 and s > 0 and s // GROUPS + 4 - 1 < TILES:
-                load(s // GROUPS + 4 - 1)
-            if s < len(steps):
-                i, b = steps[s]
-                if 25 <= s < 49:
-                    engine = 0 if s % 4 == 3 else 1
-                elif s >= 80:
-                    engine = s % 2
-                else:
-                    engine = s % 2
-                turn(i, b, engine)
+        for s in range(last + 1):
+            i, b = divmod(s, GROUPS)
+            if b == 0 and 1 <= i <= TURNED - 3:
+                if i + 2 in (8, 10):
+                    load_direct((8, 10).index(i + 2))
+                load(i + 2)
+            if i < TURNED:
+                turn(i, b)
             for act, args in at.get(s, []):
                 act(*args)

@@ -20,7 +20,7 @@ GROUPS = 8
 FREQ_PER_GROUP = FREQ // GROUPS
 WORDS = FREQ // 2
 WORDS_PER_GROUP = WORDS // GROUPS
-HALF = P // 2
+CHUNKS = ((0, 64, 8), (64, 128, 10))
 ROW_BYTES = SEG * FREQ * 2
 
 FLOPS = 2 * N_IMG * FILT * CH * FREQ
@@ -37,11 +37,12 @@ def tile_convdct_pa_kernel(tc, x_dct, k_dct, out):
         const = ctx.enter_context(tc.tile_pool(name="const", bufs=1))
         rawp = ctx.enter_context(tc.tile_pool(name="rawp", bufs=3))
         grp = ctx.enter_context(tc.tile_pool(name="grp", bufs=10))
+        hp = ctx.enter_context(tc.tile_pool(name="hp", bufs=2))
         keep = ctx.enter_context(tc.tile_pool(name="keep", bufs=1))
         xq = ctx.enter_context(tc.tile_pool(name="xq", bufs=3))
         outp = ctx.enter_context(tc.tile_pool(name="outp", bufs=1))
-        tps = ctx.enter_context(tc.psum_pool(name="tps", bufs=5))
-        mps = ctx.enter_context(tc.psum_pool(name="mps", bufs=3))
+        tps = ctx.enter_context(tc.psum_pool(name="tps", bufs=8))
+        mps = tps
 
         ident = const.tile([P, P], F32, name="ident")
         make_identity(nc, ident[:])
@@ -52,10 +53,11 @@ def tile_convdct_pa_kernel(tc, x_dct, k_dct, out):
         groups = {}
         codes = {}
         outs = {}
+        late = []
         given = {"V": 0, "S": 0}
 
         def lighter(columns):
-            engine = "V" if given["V"] <= given["S"] else "S"
+            engine = "V" if given["V"] <= given["S"] + 1024 else "S"
             given[engine] += columns
             return engine
 
@@ -75,10 +77,9 @@ def tile_convdct_pa_kernel(tc, x_dct, k_dct, out):
         def load_direct(h):
             if h == 0:
                 raws[TURNED] = rawp.tile([P, P, FREQ], BF16, name="direct", tag="direct", offset=3 * ROW_BYTES, bufs=1)
-            r0 = (TURNED - TILES_PER_UNIT) * P + h * HALF
-            nc.sync.dma_start(
-                out=raws[TURNED][:, h * HALF : (h + 1) * HALF, :], in_=x_channels[:, r0 : r0 + HALF, :]
-            )
+            c0, c1, before = CHUNKS[h]
+            r0 = (TURNED - TILES_PER_UNIT) * P
+            nc.sync.dma_start(out=raws[TURNED][:, c0:c1, :], in_=x_channels[:, r0 + c0 : r0 + c1, :])
 
         def group_dst(u, b, c0, c1):
             if (u, b) not in groups:
@@ -88,18 +89,33 @@ def tile_convdct_pa_kernel(tc, x_dct, k_dct, out):
         def turn(i, b):
             u, j = divmod(i, TILES_PER_UNIT)
             words = raws[i][:].bitcast(F32).rearrange("r (q w) -> r w q", w=WORDS)
-            bank = tps.tile([P, WORDS_PER_GROUP * P], F32, name="bank", tag="bank")
+            bank = tps.tile([P, WORDS_PER_GROUP * P], F32, name="bank", tag="ps")
             for g in range(WORDS_PER_GROUP):
                 nc.tensor.transpose(bank[:, g * P : (g + 1) * P], words[:, WORDS_PER_GROUP * b + g, :], ident[:])
             dst = group_dst(u, b, j * P, (j + 1) * P).rearrange("q (j e) r -> q j e r", e=2)
             src = bank[:].bitcast(BF16).rearrange("q (j r e) -> q j e r", j=WORDS_PER_GROUP, e=2)
             copy(lighter(2 * WORDS_PER_GROUP * P), dst, src)
 
+        def turn_held(i, b):
+            u, j = divmod(i, TILES_PER_UNIT)
+            words = raws[i][:].bitcast(F32).rearrange("r (q w) -> r w q", w=WORDS)
+            bank = tps.tile([P, WORDS_PER_GROUP * P], F32, name="bank", tag="ps")
+            for g in range(WORDS_PER_GROUP):
+                nc.tensor.transpose(bank[:, g * P : (g + 1) * P], words[:, WORDS_PER_GROUP * b + g, :], ident[:])
+            held = hp.tile([P, WORDS_PER_GROUP * P], F32, name="held", tag="held")
+            copy(lighter(WORDS_PER_GROUP * P), held[:], bank[:])
+            nc.gpsimd.tensor_scalar(
+                out=group_dst(u, b, j * P, (j + 1) * P).rearrange("q (j e) r -> q j e r", e=2),
+                in0=held[:].bitcast(BF16).rearrange("q (j r e) -> q j e r", j=WORDS_PER_GROUP, e=2),
+                scalar1=1.0, scalar2=0.0, op0=mybir.AluOpType.mult, op1=mybir.AluOpType.add
+            )
+
         def spread(b, h):
-            c0 = (TURNED % TILES_PER_UNIT) * P + h * HALF
-            dst = group_dst(TURNED // TILES_PER_UNIT, b, c0, c0 + HALF).rearrange("q (v i) r -> q v r i", i=4)
+            c0, c1, before = CHUNKS[h]
+            j0 = (TURNED % TILES_PER_UNIT) * P
+            dst = group_dst(TURNED // TILES_PER_UNIT, b, j0 + c0, j0 + c1).rearrange("q (v i) r -> q v r i", i=4)
             freqs = slice(FREQ_PER_GROUP * b, FREQ_PER_GROUP * (b + 1))
-            src = raws[TURNED][:, h * HALF : (h + 1) * HALF, freqs].rearrange("q r (v i) -> q v r i", i=4)
+            src = raws[TURNED][:, c0:c1, freqs].rearrange("q r (v i) -> q v r i", i=4)
             nc.gpsimd.tensor_scalar(
                 out=dst, in0=src, scalar1=1.0, scalar2=0.0, op0=mybir.AluOpType.mult, op1=mybir.AluOpType.add
             )
@@ -124,7 +140,7 @@ def tile_convdct_pa_kernel(tc, x_dct, k_dct, out):
                 else:
                     outs[u] = rawp.tile([P, FILT, FREQ], F32, name="out_2", tag="out_2", offset=2 * ROW_BYTES, bufs=1)
             for c in range(2):
-                acc = mps.tile([P, 4 * FILT], F32, name="acc", tag="acc")
+                acc = mps.tile([P, 4 * FILT], F32, name="acc", tag="ps")
                 for g in range(4):
                     pl = 4 * c + g
                     p = FREQ_PER_GROUP * b + pl
@@ -138,38 +154,53 @@ def tile_convdct_pa_kernel(tc, x_dct, k_dct, out):
                         stop=True,
                     )
                 p0 = FREQ_PER_GROUP * b + 4 * c
-                copy(lighter(4 * FILT), outs[u][:, :, p0 : p0 + 4], acc[:].rearrange("n (g f) -> n f g", g=4))
+                dst, src = outs[u][:, :, p0 : p0 + 4], acc[:].rearrange("n (g f) -> n f g", g=4)
+                if u == 2 and b >= 6:
+                    copy(lighter(2 * FILT), dst[:, : FILT // 2, :], src[:, : FILT // 2, :])
+                    late.append((dst[:, FILT // 2 :, :], src[:, FILT // 2 :, :]))
+                else:
+                    copy(lighter(4 * FILT), dst, src)
 
-        def store(u):
+        def store(u, s):
             n0 = (u - 1) * P
             flat = outs[u][:].rearrange("n f p -> n (f p)")
             half = FILT * FREQ // 2
-            for s in range(2):
-                nc.sync.dma_start(out=out_rows[n0 : n0 + P, s * half : (s + 1) * half], in_=flat[:, s * half : (s + 1) * half])
+            nc.sync.dma_start(out=out_rows[n0 : n0 + P, s * half : (s + 1) * half], in_=flat[:, s * half : (s + 1) * half])
+
+        def more(i):
+            for h, (c0, c1, before) in enumerate(CHUNKS):
+                if before == i:
+                    load_direct(h)
+            if i < TURNED:
+                load(i)
 
         at = {}
         for b in range(GROUPS):
             at.setdefault(25 + (4 * b) // 2, []).append((quantise, (0, b)))
             at.setdefault(57 + (5 * b) // 2, []).append((quantise, (1, b)))
             at.setdefault(61 + (5 * b) // 2, []).append((multiply, (1, b)))
-            for h in range(2):
+            for h in range(len(CHUNKS)):
                 at.setdefault(73 + h, []).append((spread, (b, h)))
             at.setdefault(81 + b, []).append((quantise, (2, b)))
             at.setdefault(84 + b, []).append((multiply, (2, b)))
-        at.setdefault(84, []).append((store, (1,)))
+        at.setdefault(84, []).extend([(store, (1, 0)), (store, (1, 1))])
         last = max(at)
-        at[last].append((store, (2,)))
+        at[last].append((store, (2, 0)))
 
         ctx.enter_context(tc.manual_schedule())
         for i in range(3):
             load(i)
         for s in range(last + 1):
             i, b = divmod(s, GROUPS)
-            if b == 0 and 1 <= i <= TURNED - 3:
-                if i + 2 in (8, 10):
-                    load_direct((8, 10).index(i + 2))
-                load(i + 2)
+            if b == 0 and 1 <= i <= TURNED - 2:
+                more(i + 2)
             if i < TURNED:
-                turn(i, b)
+                if i in (5, 6) and b in (1, 5):
+                    turn_held(i, b)
+                else:
+                    turn(i, b)
             for act, args in at.get(s, []):
                 act(*args)
+        for dst, src in late:
+            copy(lighter(2 * FILT), dst, src)
+        store(2, 1)

@@ -53,7 +53,6 @@ def tile_convdct_pa_kernel(tc, x_dct, k_dct, out):
         groups = {}
         codes = {}
         outs = {}
-        late = []
         given = {"V": 0, "S": 0}
 
         def lighter(columns):
@@ -127,10 +126,38 @@ def tile_convdct_pa_kernel(tc, x_dct, k_dct, out):
                 cols = slice(b * FREQ_PER_GROUP * P, (b + 1) * FREQ_PER_GROUP * P)
                 nc.vector.quantize_mx(out=k_codes[:, cols].bitcast(FP8X4), scales=k_scales[:, cols], in_=flat)
             else:
-                x_codes = xq.tile([P, FREQ_PER_GROUP * P], U32, name="x_codes", tag="xc", align_bytes=64)
-                x_scales = xq.tile([P, FREQ_PER_GROUP * P], U8, name="x_scales", tag="xs", align_bytes=64)
+                if u == 2 and b >= 3:
+                    slot, place = divmod(b - 3, 3)
+                    start = slot * ROW_BYTES + place * 5 * FREQ_PER_GROUP * P
+                    x_codes = rawp.tile([P, FREQ_PER_GROUP * P], U32, name="x_codes", tag="xc%d" % b, offset=start, bufs=1)
+                    x_scales = rawp.tile(
+                        [P, FREQ_PER_GROUP * P], U8, name="x_scales", tag="xs%d" % b,
+                        offset=start + 4 * FREQ_PER_GROUP * P, bufs=1,
+                    )
+                else:
+                    x_codes = xq.tile([P, FREQ_PER_GROUP * P], U32, name="x_codes", tag="xc", align_bytes=64)
+                    x_scales = xq.tile([P, FREQ_PER_GROUP * P], U8, name="x_scales", tag="xs", align_bytes=64)
                 codes[(u, b)] = (x_codes, x_scales)
                 nc.vector.quantize_mx(out=x_codes[:].bitcast(FP8X4), scales=x_scales[:], in_=flat)
+
+        def multiply_late(b):
+            x_codes, x_scales = codes[(2, b)]
+            f0 = FILT // 2
+            acc = mps.tile([P, FREQ_PER_GROUP * f0], F32, name="acc", tag="ps")
+            for g in range(FREQ_PER_GROUP):
+                p = FREQ_PER_GROUP * b + g
+                nc.tensor.matmul_mx(
+                    out=acc[:, g * f0 : (g + 1) * f0],
+                    lhsT=x_codes[:, g * P : (g + 1) * P].bitcast(FP8X4),
+                    lhsT_scale=x_scales[:, g * P : (g + 1) * P],
+                    rhs=k_codes[:, p * FILT + f0 : (p + 1) * FILT].bitcast(FP8X4),
+                    rhs_scale=k_scales[:, p * FILT + f0 : (p + 1) * FILT],
+                    start=True,
+                    stop=True,
+                )
+            freqs = slice(FREQ_PER_GROUP * b, FREQ_PER_GROUP * (b + 1))
+            dst = outs[2][:, f0:, freqs].rearrange("n f (v g) -> n v f g", g=4)
+            copy(lighter(4 * FILT), dst, acc[:].rearrange("n (v g f) -> n v f g", v=2, g=4))
 
         def multiply(u, b):
             x_codes, x_scales = codes[(u, b)]
@@ -154,12 +181,9 @@ def tile_convdct_pa_kernel(tc, x_dct, k_dct, out):
                         stop=True,
                     )
                 p0 = FREQ_PER_GROUP * b + 4 * c
-                dst, src = outs[u][:, :, p0 : p0 + 4], acc[:].rearrange("n (g f) -> n f g", g=4)
-                if u == 2 and b >= 6:
-                    copy(lighter(2 * FILT), dst[:, : FILT // 2, :], src[:, : FILT // 2, :])
-                    late.append((dst[:, FILT // 2 :, :], src[:, FILT // 2 :, :]))
-                else:
-                    copy(lighter(4 * FILT), dst, src)
+                filters = FILT if u == 1 else FILT // 2
+                dst = outs[u][:, :filters, p0 : p0 + 4]
+                copy(lighter(4 * filters), dst, acc[:].rearrange("n (g f) -> n f g", g=4)[:, :filters, :])
 
         def store(u, s):
             n0 = (u - 1) * P
@@ -182,10 +206,12 @@ def tile_convdct_pa_kernel(tc, x_dct, k_dct, out):
             for h in range(len(CHUNKS)):
                 at.setdefault(73 + h, []).append((spread, (b, h)))
             at.setdefault(81 + b, []).append((quantise, (2, b)))
-            at.setdefault(84 + b, []).append((multiply, (2, b)))
+            at.setdefault(85 + b, []).append((multiply, (2, b)))
         at.setdefault(84, []).extend([(store, (1, 0)), (store, (1, 1))])
         last = max(at)
         at[last].append((store, (2, 0)))
+        at[last].extend((multiply_late, (b,)) for b in range(GROUPS))
+        at[last].append((store, (2, 1)))
 
         ctx.enter_context(tc.manual_schedule())
         for i in range(3):
@@ -201,6 +227,3 @@ def tile_convdct_pa_kernel(tc, x_dct, k_dct, out):
                     turn(i, b)
             for act, args in at.get(s, []):
                 act(*args)
-        for dst, src in late:
-            copy(lighter(2 * FILT), dst, src)
-        store(2, 1)

from contextlib import ExitStack

import concourse.mybir as mybir
from concourse.masks import make_identity

F32 = mybir.dt.float32
BF16 = mybir.dt.bfloat16
U32 = mybir.dt.uint32
U8 = mybir.dt.uint8
FP8X4 = mybir.dt.float8_e4m3fn_x4

N_IMG, CH, FILT, FREQ = 256, 512, 128, 64
P = 128
PACK = 4
SEG = CH // PACK
TILES_PER_UNIT = 4
TILES = 12
TURNED = TILES - 1
GROUPS = 8
FREQ_PER_GROUP = FREQ // GROUPS
WORDS = FREQ // 2
WORDS_PER_GROUP = WORDS // GROUPS
CHUNKS = ((0, 64, 8), (64, 128, 10))
ROW_BYTES = SEG * FREQ * 2

FLOPS = 2 * N_IMG * FILT * CH * FREQ


def tile_convdct_pa_kernel(tc, x_dct, k_dct, out):
    nc = tc.nc
    x_rows = x_dct.rearrange("n (t q) h w -> (n t) (q h w)", t=PACK)
    k_rows = k_dct.rearrange("n (t q) h w -> (n t) (q h w)", t=PACK)
    x_channels = x_dct.rearrange("n (t q) h w -> q (n t) (h w)", t=PACK)
    out_rows = out.rearrange("n f h w -> n (f h w)")

    with ExitStack() as ctx:
        const = ctx.enter_context(tc.tile_pool(name="const", bufs=1))
        rawp = ctx.enter_context(tc.tile_pool(name="rawp", bufs=3))
        grp = ctx.enter_context(tc.tile_pool(name="grp", bufs=10))
        hp = ctx.enter_context(tc.tile_pool(name="hp", bufs=2))
        keep = ctx.enter_context(tc.tile_pool(name="keep", bufs=1))
        xq = ctx.enter_context(tc.tile_pool(name="xq", bufs=3))
        outp = ctx.enter_context(tc.tile_pool(name="outp", bufs=1))
        tps = ctx.enter_context(tc.psum_pool(name="tps", bufs=8))
        mps = tps

        ident = const.tile([P, P], F32, name="ident")
        make_identity(nc, ident[:])
        k_codes = keep.tile([P, FREQ * FILT], U32, name="k_codes", align_bytes=64)
        k_scales = keep.tile([P, FREQ * FILT], U8, name="k_scales", align_bytes=64)

        raws = {}
        groups = {}
        codes = {}
        outs = {}
        given = {"V": 0, "S": 0}

        def lighter(columns):
            engine = "V" if given["V"] <= given["S"] + 1024 else "S"
            given[engine] += columns
            return engine

        def copy(engine, dst, src):
            if engine == "V":
                nc.vector.tensor_copy(out=dst, in_=src)
            else:
                nc.scalar.copy(out=dst, in_=src)

        def load(i):
            slot = i % 3
            raws[i] = rawp.tile([P, SEG * FREQ], BF16, name="raw", tag="raw%d" % slot, offset=slot * ROW_BYTES, bufs=1)
            rows = k_rows if i < TILES_PER_UNIT else x_rows
            r0 = (i % TILES_PER_UNIT if i < TILES_PER_UNIT else i - TILES_PER_UNIT) * P
            nc.sync.dma_start(out=raws[i][:], in_=rows[r0 : r0 + P, :])

        def load_direct(h):
            if h == 0:
                raws[TURNED] = rawp.tile([P, P, FREQ], BF16, name="direct", tag="direct", offset=3 * ROW_BYTES, bufs=1)
            c0, c1, before = CHUNKS[h]
            r0 = (TURNED - TILES_PER_UNIT) * P
            nc.sync.dma_start(out=raws[TURNED][:, c0:c1, :], in_=x_channels[:, r0 + c0 : r0 + c1, :])

        def group_dst(u, b, c0, c1):
            if (u, b) not in groups:
                groups[(u, b)] = grp.tile([P, FREQ_PER_GROUP, PACK * P], BF16, name="g", tag="g", align_bytes=64)
            return groups[(u, b)][:, :, c0:c1]

        def turn(i, b):
            u, j = divmod(i, TILES_PER_UNIT)
            words = raws[i][:].bitcast(F32).rearrange("r (q w) -> r w q", w=WORDS)
            bank = tps.tile([P, WORDS_PER_GROUP * P], F32, name="bank", tag="ps")
            for g in range(WORDS_PER_GROUP):
                nc.tensor.transpose(bank[:, g * P : (g + 1) * P], words[:, WORDS_PER_GROUP * b + g, :], ident[:])
            dst = group_dst(u, b, j * P, (j + 1) * P).rearrange("q (j e) r -> q j e r", e=2)
            src = bank[:].bitcast(BF16).rearrange("q (j r e) -> q j e r", j=WORDS_PER_GROUP, e=2)
            copy(lighter(2 * WORDS_PER_GROUP * P), dst, src)

        def turn_held(i, b):
            u, j = divmod(i, TILES_PER_UNIT)
            words = raws[i][:].bitcast(F32).rearrange("r (q w) -> r w q", w=WORDS)
            bank = tps.tile([P, WORDS_PER_GROUP * P], F32, name="bank", tag="ps")
            for g in range(WORDS_PER_GROUP):
                nc.tensor.transpose(bank[:, g * P : (g + 1) * P], words[:, WORDS_PER_GROUP * b + g, :], ident[:])
            held = hp.tile([P, WORDS_PER_GROUP * P], F32, name="held", tag="held")
            copy(lighter(WORDS_PER_GROUP * P), held[:], bank[:])
            nc.gpsimd.tensor_scalar(
                out=group_dst(u, b, j * P, (j + 1) * P).rearrange("q (j e) r -> q j e r", e=2),
                in0=held[:].bitcast(BF16).rearrange("q (j r e) -> q j e r", j=WORDS_PER_GROUP, e=2),
                scalar1=1.0, scalar2=0.0, op0=mybir.AluOpType.mult, op1=mybir.AluOpType.add
            )

        def spread(b, h):
            c0, c1, before = CHUNKS[h]
            j0 = (TURNED % TILES_PER_UNIT) * P
            dst = group_dst(TURNED // TILES_PER_UNIT, b, j0 + c0, j0 + c1).rearrange("q (v i) r -> q v r i", i=4)
            freqs = slice(FREQ_PER_GROUP * b, FREQ_PER_GROUP * (b + 1))
            src = raws[TURNED][:, c0:c1, freqs].rearrange("q r (v i) -> q v r i", i=4)
            nc.gpsimd.tensor_scalar(
                out=dst, in0=src, scalar1=1.0, scalar2=0.0, op0=mybir.AluOpType.mult, op1=mybir.AluOpType.add
            )

        def quantise(u, b):
            given["V"] += FREQ_PER_GROUP * P
            flat = groups[(u, b)][:].rearrange("q p r -> q (p r)")
            if u == 0:
                cols = slice(b * FREQ_PER_GROUP * P, (b + 1) * FREQ_PER_GROUP * P)
                nc.vector.quantize_mx(out=k_codes[:, cols].bitcast(FP8X4), scales=k_scales[:, cols], in_=flat)
            else:
                if u == 2 and b >= 3:
                    slot, place = divmod(b - 3, 3)
                    start = slot * ROW_BYTES + place * 5 * FREQ_PER_GROUP * P
                    x_codes = rawp.tile([P, FREQ_PER_GROUP * P], U32, name="x_codes", tag="xc%d" % b, offset=start, bufs=1)
                    x_scales = rawp.tile(
                        [P, FREQ_PER_GROUP * P], U8, name="x_scales", tag="xs%d" % b,
                        offset=start + 4 * FREQ_PER_GROUP * P, bufs=1,
                    )
                else:
                    x_codes = xq.tile([P, FREQ_PER_GROUP * P], U32, name="x_codes", tag="xc", align_bytes=64)
                    x_scales = xq.tile([P, FREQ_PER_GROUP * P], U8, name="x_scales", tag="xs", align_bytes=64)
                codes[(u, b)] = (x_codes, x_scales)
                nc.vector.quantize_mx(out=x_codes[:].bitcast(FP8X4), scales=x_scales[:], in_=flat)

        def multiply_late(b):
            x_codes, x_scales = codes[(2, b)]
            f0 = FILT // 2
            acc = mps.tile([P, FREQ_PER_GROUP * f0], F32, name="acc", tag="ps")
            for g in range(FREQ_PER_GROUP):
                p = FREQ_PER_GROUP * b + g
                nc.tensor.matmul_mx(
                    out=acc[:, g * f0 : (g + 1) * f0],
                    lhsT=x_codes[:, g * P : (g + 1) * P].bitcast(FP8X4),
                    lhsT_scale=x_scales[:, g * P : (g + 1) * P],
                    rhs=k_codes[:, p * FILT + f0 : (p + 1) * FILT].bitcast(FP8X4),
                    rhs_scale=k_scales[:, p * FILT + f0 : (p + 1) * FILT],
                    start=True,
                    stop=True,
                )
            freqs = slice(FREQ_PER_GROUP * b, FREQ_PER_GROUP * (b + 1))
            dst = outs[2][:, f0:, freqs].rearrange("n f (v g) -> n v f g", g=4)
            copy(lighter(4 * FILT), dst, acc[:].rearrange("n (v g f) -> n v f g", v=2, g=4))

        def multiply(u, b):
            x_codes, x_scales = codes[(u, b)]
            if b == 0:
                if u == 1:
                    outs[u] = outp.tile([P, FILT, FREQ], F32, name="out_1", tag="out_1")
                else:
                    outs[u] = rawp.tile([P, FILT, FREQ], F32, name="out_2", tag="out_2", offset=2 * ROW_BYTES, bufs=1)
            for c in range(2):
                acc = mps.tile([P, 4 * FILT], F32, name="acc", tag="ps")
                for g in range(4):
                    pl = 4 * c + g
                    p = FREQ_PER_GROUP * b + pl
                    nc.tensor.matmul_mx(
                        out=acc[:, g * FILT : (g + 1) * FILT],
                        lhsT=x_codes[:, pl * P : (pl + 1) * P].bitcast(FP8X4),
                        lhsT_scale=x_scales[:, pl * P : (pl + 1) * P],
                        rhs=k_codes[:, p * FILT : (p + 1) * FILT].bitcast(FP8X4),
                        rhs_scale=k_scales[:, p * FILT : (p + 1) * FILT],
                        start=True,
                        stop=True,
                    )
                p0 = FREQ_PER_GROUP * b + 4 * c
                filters = FILT if u == 1 else FILT // 2
                dst = outs[u][:, :filters, p0 : p0 + 4]
                copy(lighter(4 * filters), dst, acc[:].rearrange("n (g f) -> n f g", g=4)[:, :filters, :])

        def store(u, s):
            n0 = (u - 1) * P
            flat = outs[u][:].rearrange("n f p -> n (f p)")
            half = FILT * FREQ // 2
            nc.sync.dma_start(out=out_rows[n0 : n0 + P, s * half : (s + 1) * half], in_=flat[:, s * half : (s + 1) * half])

        def more(i):
            for h, (c0, c1, before) in enumerate(CHUNKS):
                if before == i:
                    load_direct(h)
            if i < TURNED:
                load(i)

        at = {}
        for b in range(GROUPS):
            at.setdefault(25 + (4 * b) // 2, []).append((quantise, (0, b)))
            at.setdefault(57 + (5 * b) // 2, []).append((quantise, (1, b)))
            at.setdefault(61 + (5 * b) // 2, []).append((multiply, (1, b)))
            for h in range(len(CHUNKS)):
                at.setdefault(73 + h, []).append((spread, (b, h)))
            at.setdefault(81 + b, []).append((quantise, (2, b)))
            at.setdefault(85 + b, []).append((multiply, (2, b)))
        at.setdefault(84, []).extend([(store, (1, 0)), (store, (1, 1))])
        last = max(at)
        at[last].append((store, (2, 0)))
        at[last].extend((multiply_late, (b,)) for b in range(GROUPS))
        at[last].append((store, (2, 1)))

        ctx.enter_context(tc.manual_schedule())
        for i in range(3):
            load(i)
        for s in range(last + 1):
            i, b = divmod(s, GROUPS)
            if b == 0 and 1 <= i <= TURNED - 2:
                more(i + 2)
            if i < TURNED:
                if i in (5, 6) and b in (1, 5):
                    turn_held(i, b)
                else:
                    turn(i, b)
            for act, args in at.get(s, []):
                act(*args)
